import numpy as np
import ml_dtypes


def mxq(x, axis, fmt="e4m3"):
    dtype, down = {"e4m3": (ml_dtypes.float8_e4m3fn, 7), "e5m2": (ml_dtypes.float8_e5m2, 14)}[fmt]
    v = np.moveaxis(np.asarray(x, np.float32).astype(ml_dtypes.bfloat16).astype(np.float64), axis, -1)
    blocks = v.reshape(v.shape[:-1] + (-1, 32))
    amax = np.abs(blocks).max(-1, keepdims=True)
    byte = np.maximum(np.where(amax > 0, np.frexp(amax)[1] - 1 + 127, 0) - down, 1)
    scale = np.exp2(byte - 127.0)
    codes = (blocks / scale).astype(np.float32).astype(dtype).astype(np.float64)
    return np.moveaxis((codes * scale).reshape(v.shape), -1, axis)


WIDE = False


def mx_kscale(k):
    if not WIDE:
        return np.ones(k)
    levels = np.array([10, -10, 5, -5, 0])
    a = np.random.permutation(np.resize(levels, k // 512 * 4)).reshape(k // 512, 4)
    idx = np.arange(k)
    return np.exp2(a[idx // 512, idx % 128 // 32])


BF16 = ml_dtypes.bfloat16


def bf(x):
    return np.asarray(x, np.float32).astype(BF16)


def f64(x):
    return np.asarray(x).astype(np.float64)


B, S, H, HD = 1, 512, 2048, 128
NH = H // HD
HALF = HD // 2
WS = 1.5 * (HD / H) ** 0.25 / np.sqrt(H)


def rotate_half(u):
    return np.concatenate((-u[..., HALF:], u[..., :HALF]), axis=-1)


def rope(u, c, s):
    u4 = u.reshape(B, S, NH, HD)
    return (u4 * c[None, :, None, :] + rotate_half(u4) * s[None, :, None, :]).reshape(B, S, H)


def setup_inputs():
    s = mx_kscale(H)
    t = np.tile(mx_kscale(H).reshape(NH, 2, HALF)[:, :1, :], (1, 2, 1)).reshape(H)
    return {"hidden_states": bf(np.random.standard_normal((B, S, H)) * s),
            "wq_deq": bf(np.random.standard_normal((H, H)) * WS * t[:, None] / s[None, :]),
            "wk_deq": bf(np.random.standard_normal((H, H)) * WS / t[:, None] / s[None, :]),
            "cos": bf(np.random.random((S, HD))),
            "sin": bf(np.random.random((S, HD))),
            "attention_mask": bf(np.random.standard_normal((1, S, S)) * 0.5)}


def reference(hidden_states, wq_deq, wk_deq, cos, sin, attention_mask):
    xq = mxq(f64(hidden_states), 2, "e4m3")
    q = xq @ mxq(f64(wq_deq), 1, "e4m3").T
    k = xq @ mxq(f64(wk_deq), 1, "e4m3").T
    q_rot = rope(q, f64(cos), f64(sin))
    k_rot = rope(k, f64(cos), f64(sin))
    scores = (mxq(q_rot, 2, "e4m3") @ mxq(k_rot, 2, "e4m3").transpose(0, 2, 1)) / np.sqrt(HD)
    return scores + f64(attention_mask)

@@ -1,0 +1,324 @@
+import math
+from contextlib import ExitStack
+
+import concourse.mybir as mybir
+from concourse.masks import make_identity
+
+BF16 = mybir.dt.bfloat16
+F32 = mybir.dt.float32
+U32 = mybir.dt.uint32
+U8 = mybir.dt.uint8
+FP8X4 = mybir.dt.float8_e4m3fn_x4
+MULT = mybir.AluOpType.mult
+ADD = mybir.AluOpType.add
+
+P = 128
+S = 512
+H = 2048
+HD = 128
+HALF = HD // 2
+PACK = 4
+K_PASS = P * PACK
+PASSES = H // K_PASS
+S_TILES = S // P
+PAIR_ROWS = 2 * HD
+UNITS = 2 * H // PAIR_ROWS
+UNIT_COLS = PASSES * 2 * P
+LOADS_AHEAD = 4
+SUM_PIECES = 2
+
+COS_LO, SIN_HI, COS_HI, NEG_SIN_LO = 0, 1, 2, 3
+
+FLOPS = 2 * (2 * S * H * H) + 2 * S * S * H
+
+
+def tile_llamaattention_pa_kernel(
+    tc, hidden_states, wq_deq, wk_deq, cos, sin, attention_mask, out
+):
+    nc = tc.nc
+    x_rows = hidden_states.flatten_outer_dims()
+    mask_rows = attention_mask.flatten_outer_dims()
+    out_rows = out.flatten_outer_dims()
+    weights = (wq_deq, wk_deq)
+
+    with ExitStack() as ctx:
+        keep = ctx.enter_context(tc.tile_pool(name="keep", bufs=1))
+        raw_pool = ctx.enter_context(tc.tile_pool(name="raw", bufs=LOADS_AHEAD))
+        grouped_pool = ctx.enter_context(tc.tile_pool(name="grouped", bufs=2))
+        codes_pool = ctx.enter_context(tc.tile_pool(name="codes", bufs=2))
+        rope_pool = ctx.enter_context(tc.tile_pool(name="rope", bufs=3))
+        rot_pool = ctx.enter_context(tc.tile_pool(name="rot", bufs=3))
+        out_pool = ctx.enter_context(tc.tile_pool(name="outp", bufs=S_TILES))
+        turn_psum = ctx.enter_context(tc.psum_pool(name="turn", bufs=4))
+        acc_psum = ctx.enter_context(tc.psum_pool(name="acc", bufs=4))
+        ctx.enter_context(tc.manual_schedule())
+
+        cos_sb = keep.tile([P, S_TILES * HD], BF16, name="cos_sb")
+        sin_sb = keep.tile([P, S_TILES * HD], BF16, name="sin_sb")
+        nc.scalar.dma_start(
+            out=cos_sb[:].rearrange("p (r d) -> p r d", r=S_TILES),
+            in_=cos.rearrange("(r p) d -> p r d", p=P),
+        )
+        nc.scalar.dma_start(
+            out=sin_sb[:].rearrange("p (r d) -> p r d", r=S_TILES),
+            in_=sin.rearrange("(r p) d -> p r d", p=P),
+        )
+
+        x_raw = keep.tile([P, S_TILES * H], BF16, name="x_raw")
+        for r in range(S_TILES):
+            nc.sync.dma_start(
+                out=x_raw[:, r * H : (r + 1) * H], in_=x_rows[r * P : (r + 1) * P, :]
+            )
+
+        raw_tiles = {}
+
+        def load_weights(n):
+            which = (n % 4) // 2
+            row0 = (2 * (n // 4) + n % 2) * PAIR_ROWS
+            w_raw = raw_pool.tile([P, 2 * H], BF16, name="w_raw", tag="w_raw")
+            nc.sync.dma_start(
+                out=w_raw[:].rearrange("p (c k) -> p c k", c=2),
+                in_=weights[which][row0 : row0 + PAIR_ROWS, :].rearrange(
+                    "(c p) k -> p c k", p=P
+                ),
+            )
+            raw_tiles[n] = w_raw
+
+        for n in range(LOADS_AHEAD):
+            load_weights(n)
+
+        ident_f32 = keep.tile([P, P], F32, name="ident_f32")
+        make_identity(nc, ident_f32[:])
+        ident_bf16 = keep.tile([P, P], BF16, name="ident_bf16")
+        make_identity(nc, ident_bf16[:])
+
+        doubled = keep.tile([P, S_TILES * 4 * P], BF16, name="doubled")
+        doubled_halves = doubled[:].rearrange(
+            "p (r t c d) -> p r t c d", r=S_TILES, t=4, c=2
+        )
+        cos_halves = cos_sb[:].rearrange("p (r h d) -> p r h d", r=S_TILES, h=2)
+        sin_halves = sin_sb[:].rearrange("p (r h d) -> p r h d", r=S_TILES, h=2)
+        twice = [P, S_TILES, 2, HALF]
+        nc.vector.tensor_copy(
+            out=doubled_halves[:, :, COS_LO, :, :],
+            in_=cos_halves[:, :, 0, :].unsqueeze(2).to_broadcast(twice),
+        )
+        nc.vector.tensor_copy(
+            out=doubled_halves[:, :, SIN_HI, :, :],
+            in_=sin_halves[:, :, 1, :].unsqueeze(2).to_broadcast(twice),
+        )
+        nc.vector.tensor_copy(
+            out=doubled_halves[:, :, COS_HI, :, :],
+            in_=cos_halves[:, :, 1, :].unsqueeze(2).to_broadcast(twice),
+        )
+        nc.vector.tensor_scalar_mul(
+            out=doubled_halves[:, :, NEG_SIN_LO, :, :],
+            in0=sin_halves[:, :, 0, :].unsqueeze(2).to_broadcast(twice),
+            scalar1=-1.0,
+        )
+        doubled_tiles = doubled[:].rearrange("p (r t f) -> p r t f", r=S_TILES, t=4)
+        tables = keep.tile([P, 4, S], BF16, name="tables")
+        for b in range(2):
+            tables_t = acc_psum.tile([P, 2, S], BF16, name="tables_t", tag="acc")
+            for t in range(2):
+                for r in range(S_TILES):
+                    nc.tensor.transpose(
+                        tables_t[:, t, r * P : (r + 1) * P],
+                        doubled_tiles[:, r, 2 * b + t, :],
+                        ident_bf16[:],
+                    )
+            nc.scalar.copy(out=tables[:, 2 * b : 2 * b + 2, :], in_=tables_t[:])
+
+        x_words = x_raw[:].bitcast(F32).rearrange("p (r w) -> p r w", r=S_TILES)
+        x_grouped = keep.tile([P, PASSES * S * PACK], BF16, name="x_grouped", align_bytes=64)
+        x_grouped_words = x_grouped[:].bitcast(F32).rearrange(
+            "p (g s u) -> p g s u", g=PASSES, u=2
+        )
+        x_codes = keep.tile([P, PASSES * S], U32, name="x_codes", align_bytes=64)
+        x_scales = keep.tile([P, PASSES * S], U8, name="x_scales", align_bytes=64)
+
+        def turn_x(r):
+            for half in range(2):
+                x_t = acc_psum.tile([P, 2, 2, P], F32, name="x_t", tag="acc")
+                for g in range(2):
+                    for u in range(2):
+                        block = (2 * (2 * half + g) + u) * P
+                        nc.tensor.transpose(
+                            x_t[:, g, u, :], x_words[:, r, block : block + P], ident_f32[:]
+                        )
+                copy = nc.scalar.copy if half == 0 else nc.vector.tensor_copy
+                copy(
+                    out=x_grouped_words[:, 2 * half : 2 * half + 2, r * P : (r + 1) * P, :],
+                    in_=x_t[:].rearrange("p g u s -> p g s u"),
+                )
+
+        def quantise_x(r):
+            for g in range(PASSES):
+                first = g * S + r * P
+                nc.vector.quantize_mx(
+                    out=x_codes[:, first : first + P].bitcast(FP8X4),
+                    scales=x_scales[:, first : first + P],
+                    in_=x_grouped[:, first * PACK : (first + P) * PACK],
+                )
+
+        for r in range(S_TILES):
+            turn_x(r)
+            if r > 0:
+                quantise_x(r - 1)
+        quantise_x(S_TILES - 1)
+
+        w_quantised = {}
+
+        def prepare_weights(n):
+            w_words = raw_tiles[n][:].bitcast(F32).rearrange("p (c w) -> p c w", c=2)
+            w_grouped = grouped_pool.tile(
+                [P, UNIT_COLS * PACK], BF16, name="w_grouped", tag="w_grouped", align_bytes=64
+            )
+            w_grouped_words = w_grouped[:].bitcast(F32).rearrange(
+                "p (g h c d u) -> p g h c d u", g=PASSES, h=2, c=2, u=2
+            )
+            for g in range(PASSES):
+                w_t = turn_psum.tile([P, 2, 2, P], F32, name="w_t", tag="turn")
+                for c in range(2):
+                    for u in range(2):
+                        block = (2 * g + u) * P
+                        nc.tensor.transpose(
+                            w_t[:, c, u, :], w_words[:, c, block : block + P], ident_f32[:]
+                        )
+                for h in range(2):
+                    nc.scalar.copy(
+                        out=w_grouped_words[:, g, h, :, :, :],
+                        in_=w_t[:, :, :, h * HALF : (h + 1) * HALF].rearrange(
+                            "p c u d -> p c d u"
+                        ),
+                    )
+            w_codes = codes_pool.tile(
+                [P, UNIT_COLS], U32, name="w_codes", tag="w_codes", align_bytes=64
+            )
+            w_scales = codes_pool.tile(
+                [P, UNIT_COLS], U8, name="w_scales", tag="w_scales", align_bytes=64
+            )
+            nc.vector.quantize_mx(
+                out=w_codes[:].bitcast(FP8X4), scales=w_scales[:], in_=w_grouped[:]
+            )
+            w_quantised[n] = (w_codes, w_scales)
+
+        def project(n):
+            w_codes, w_scales = w_quantised[n]
+            halves = []
+            for h in range(2):
+                acc = acc_psum.tile([P, S], F32, name="acc", tag="acc")
+                for g in range(PASSES):
+                    cols = slice((2 * g + h) * P, (2 * g + h + 1) * P)
+                    nc.tensor.matmul_mx(
+                        out=acc[:],
+                        lhsT=w_codes[:, cols].bitcast(FP8X4),
+                        lhsT_scale=w_scales[:, cols],
+                        rhs=x_codes[:, g * S : (g + 1) * S].bitcast(FP8X4),
+                        rhs_scale=x_scales[:, g * S : (g + 1) * S],
+                        start=(g == 0),
+                        stop=(g == PASSES - 1),
+                    )
+                halves.append(acc)
+            return halves
+
+        rot_codes = []
+        rot_scales = []
+        for which in range(2):
+            rot_codes.append(
+                keep.tile([P, PASSES * S], U32, name="rot_codes%d" % which, align_bytes=64)
+            )
+            rot_scales.append(
+                keep.tile([P, PASSES * S], U8, name="rot_scales%d" % which, align_bytes=64)
+            )
+        rot_tiles = {}
+
+        def rope(n, lo, hi):
+            own = rope_pool.tile([P, 2, S], F32, name="own", tag="own")
+            cross = rope_pool.tile([P, 2, S], F32, name="cross", tag="cross")
+            nc.vector.tensor_tensor(
+                out=own[:, 0, :], in0=lo[:], in1=tables[:, COS_LO, :], op=MULT
+            )
+            nc.vector.tensor_tensor(
+                out=cross[:, 1, :], in0=lo[:], in1=tables[:, SIN_HI, :], op=MULT
+            )
+            nc.vector.tensor_tensor(
+                out=own[:, 1, :], in0=hi[:], in1=tables[:, COS_HI, :], op=MULT
+            )
+            nc.vector.tensor_tensor(
+                out=cross[:, 0, :], in0=hi[:], in1=tables[:, NEG_SIN_LO, :], op=MULT
+            )
+            if n % 2 == 0:
+                rot_tiles[n // 2] = rot_pool.tile(
+                    [P, S * PACK], BF16, name="rot_grouped", tag="rot_grouped", align_bytes=64
+                )
+            rot_pairs = rot_tiles[n // 2][:].rearrange("p (s j h) -> p s j h", j=2, h=2)
+            own_by_pos = own[:].rearrange("p h s -> p s h")
+            cross_by_pos = cross[:].rearrange("p h s -> p s h")
+            piece = S // SUM_PIECES
+            for i in range(SUM_PIECES):
+                span = slice(i * piece, (i + 1) * piece)
+                nc.gpsimd.tensor_tensor(
+                    out=rot_pairs[:, span, n % 2, :],
+                    in0=own_by_pos[:, span, :],
+                    in1=cross_by_pos[:, span, :],
+                    op=ADD,
+                )
+
+        def quantise_rot(pair):
+            which = pair % 2
+            cols = slice((pair // 2) * S, (pair // 2 + 1) * S)
+            nc.vector.quantize_mx(
+                out=rot_codes[which][:, cols].bitcast(FP8X4),
+                scales=rot_scales[which][:, cols],
+                in_=rot_tiles[pair][:],
+            )
+
+        prepare_weights(0)
+        for n in range(UNITS):
+            if n + LOADS_AHEAD < UNITS:
+                load_weights(n + LOADS_AHEAD)
+            if n + 1 < UNITS:
+                prepare_weights(n + 1)
+            lo, hi = project(n)
+            rope(n, lo, hi)
+            if n % 2 == 0 and n > 0:
+                quantise_rot(n // 2 - 1)
+
+        mask_sb = keep.tile([P, S_TILES, S], BF16, name="mask_sb")
+        nc.sync.dma_start(out=mask_sb[:], in_=mask_rows.rearrange("(m p) s -> p m s", p=P))
+
+        scores = []
+        for m in range(S_TILES):
+            scores.append(turn_psum.tile([P, S], F32, name="scores%d" % m, tag="turn"))
+
+        def add_scores(g):
+            for m in range(S_TILES):
+                q_cols = slice(g * S + m * P, g * S + (m + 1) * P)
+                k_cols = slice(g * S, (g + 1) * S)
+                nc.tensor.matmul_mx(
+                    out=scores[m][:],
+                    lhsT=rot_codes[0][:, q_cols].bitcast(FP8X4),
+                    lhsT_scale=rot_scales[0][:, q_cols],
+                    rhs=rot_codes[1][:, k_cols].bitcast(FP8X4),
+                    rhs_scale=rot_scales[1][:, k_cols],
+                    start=(g == 0),
+                    stop=(g == PASSES - 1),
+                )
+
+        for g in range(PASSES - 1):
+            add_scores(g)
+        quantise_rot(UNITS // 2 - 1)
+        add_scores(PASSES - 1)
+
+        for m in range(S_TILES):
+            result = out_pool.tile([P, S], F32, name="result", tag="result")
+            nc.vector.scalar_tensor_tensor(
+                out=result[:],
+                in0=scores[m][:],
+                scalar=1.0 / math.sqrt(HD),
+                in1=mask_sb[:, m, :],
+                op0=MULT,
+                op1=ADD,
+            )
+            nc.sync.dma_start(out=out_rows[m * P : (m + 1) * P, :], in_=result[:])

@@ -25,7 +25,8 @@ PAIR_ROWS = 2 * HD
 UNITS = 2 * H // PAIR_ROWS
 UNIT_COLS = PASSES * 2 * P
 LOADS_AHEAD = 4
-SUM_PIECES = 2
+UNIT_SUMS = 2 * S
+GPSIMD_SUMS = 768
 
 COS_LO, SIN_HI, COS_HI, NEG_SIN_LO = 0, 1, 2, 3
 
@@ -48,6 +49,7 @@ def tile_llamaattention_pa_kernel(
         codes_pool = ctx.enter_context(tc.tile_pool(name="codes", bufs=2))
         rope_pool = ctx.enter_context(tc.tile_pool(name="rope", bufs=3))
         rot_pool = ctx.enter_context(tc.tile_pool(name="rot", bufs=3))
+        rot_grouped_pool = ctx.enter_context(tc.tile_pool(name="rotg", bufs=2))
         out_pool = ctx.enter_context(tc.tile_pool(name="outp", bufs=S_TILES))
         turn_psum = ctx.enter_context(tc.psum_pool(name="turn", bufs=4))
         acc_psum = ctx.enter_context(tc.psum_pool(name="acc", bufs=4))
@@ -231,39 +233,53 @@ def tile_llamaattention_pa_kernel(
             rot_scales.append(
                 keep.tile([P, PASSES * S], U8, name="rot_scales%d" % which, align_bytes=64)
             )
+        product_tiles = {}
         rot_tiles = {}
+        rot_grouped_tiles = {}
 
-        def rope(n, lo, hi):
-            own = rope_pool.tile([P, 2, S], F32, name="own", tag="own")
-            cross = rope_pool.tile([P, 2, S], F32, name="cross", tag="cross")
+        def rope_products(n, lo, hi):
+            products = rope_pool.tile([P, 4, S], F32, name="products", tag="products")
             nc.vector.tensor_tensor(
-                out=own[:, 0, :], in0=lo[:], in1=tables[:, COS_LO, :], op=MULT
+                out=products[:, 0:4:3, :],
+                in0=lo[:].unsqueeze(1).to_broadcast([P, 2, S]),
+                in1=tables[:, COS_LO : SIN_HI + 1, :],
+                op=MULT,
             )
             nc.vector.tensor_tensor(
-                out=cross[:, 1, :], in0=lo[:], in1=tables[:, SIN_HI, :], op=MULT
+                out=products[:, 1:3, :],
+                in0=hi[:].unsqueeze(1).to_broadcast([P, 2, S]),
+                in1=tables[:, COS_HI : NEG_SIN_LO + 1, :],
+                op=MULT,
             )
-            nc.vector.tensor_tensor(
-                out=own[:, 1, :], in0=hi[:], in1=tables[:, COS_HI, :], op=MULT
-            )
-            nc.vector.tensor_tensor(
-                out=cross[:, 0, :], in0=hi[:], in1=tables[:, NEG_SIN_LO, :], op=MULT
-            )
+            product_tiles[n] = products
+
+        def rope_sums(n):
             if n % 2 == 0:
-                rot_tiles[n // 2] = rot_pool.tile(
-                    [P, S * PACK], BF16, name="rot_grouped", tag="rot_grouped", align_bytes=64
-                )
-            rot_pairs = rot_tiles[n // 2][:].rearrange("p (s j h) -> p s j h", j=2, h=2)
-            own_by_pos = own[:].rearrange("p h s -> p s h")
-            cross_by_pos = cross[:].rearrange("p h s -> p s h")
-            piece = S // SUM_PIECES
-            for i in range(SUM_PIECES):
-                span = slice(i * piece, (i + 1) * piece)
-                nc.gpsimd.tensor_tensor(
-                    out=rot_pairs[:, span, n % 2, :],
-                    in0=own_by_pos[:, span, :],
-                    in1=cross_by_pos[:, span, :],
-                    op=ADD,
-                )
+                rot_tiles[n // 2] = rot_pool.tile([P, PACK * S], BF16, name="rot", tag="rot")
+            first = (n % 2) * UNIT_SUMS
+            flat = product_tiles[n][:].rearrange("p t s -> p (t s)")
+            nc.gpsimd.tensor_tensor(
+                out=rot_tiles[n // 2][:, first : first + GPSIMD_SUMS],
+                in0=flat[:, 0:GPSIMD_SUMS],
+                in1=flat[:, UNIT_SUMS : UNIT_SUMS + GPSIMD_SUMS],
+                op=ADD,
+            )
+            nc.vector.tensor_tensor(
+                out=rot_tiles[n // 2][:, first + GPSIMD_SUMS : first + UNIT_SUMS],
+                in0=flat[:, GPSIMD_SUMS:UNIT_SUMS],
+                in1=flat[:, UNIT_SUMS + GPSIMD_SUMS : 2 * UNIT_SUMS],
+                op=ADD,
+            )
+
+        def group_rot(pair):
+            rot_grouped = rot_grouped_pool.tile(
+                [P, S * PACK], BF16, name="rot_grouped", tag="rot_grouped", align_bytes=64
+            )
+            nc.scalar.copy(
+                out=rot_grouped[:].rearrange("p (c i t) -> p c t i", i=4, t=PACK),
+                in_=rot_tiles[pair][:].rearrange("p (t c i) -> p c t i", t=PACK, i=4),
+            )
+            rot_grouped_tiles[pair] = rot_grouped
 
         def quantise_rot(pair):
             which = pair % 2
@@ -271,8 +287,16 @@ def tile_llamaattention_pa_kernel(
             nc.vector.quantize_mx(
                 out=rot_codes[which][:, cols].bitcast(FP8X4),
                 scales=rot_scales[which][:, cols],
-                in_=rot_tiles[pair][:],
+                in_=rot_grouped_tiles[pair][:],
             )
+
+        def finish_rope(n):
+            if 1 <= n <= UNITS:
+                rope_sums(n - 1)
+            if n % 2 == 1 and 3 <= n:
+                group_rot((n - 3) // 2)
+            if n % 2 == 0 and 4 <= n:
+                quantise_rot((n - 4) // 2)
 
         prepare_weights(0)
         for n in range(UNITS):
@@ -281,9 +305,8 @@ def tile_llamaattention_pa_kernel(
             if n + 1 < UNITS:
                 prepare_weights(n + 1)
             lo, hi = project(n)
-            rope(n, lo, hi)
-            if n % 2 == 0 and n > 0:
-                quantise_rot(n // 2 - 1)
+            finish_rope(n)
+            rope_products(n, lo, hi)
 
         mask_sb = keep.tile([P, S_TILES, S], BF16, name="mask_sb")
         nc.sync.dma_start(out=mask_sb[:], in_=mask_rows.rearrange("(m p) s -> p m s", p=P))
@@ -308,7 +331,8 @@ def tile_llamaattention_pa_kernel(
 
         for g in range(PASSES - 1):
             add_scores(g)
-        quantise_rot(UNITS // 2 - 1)
+        for n in range(UNITS, UNITS + 3):
+            finish_rope(n)
         add_scores(PASSES - 1)
 
         for m in range(S_TILES):

@@ -25,6 +25,9 @@ PAIR_ROWS = 2 * HD
 UNITS = 2 * H // PAIR_ROWS
 UNIT_COLS = PASSES * 2 * P
 LOADS_AHEAD = 4
+RUN_BANKS = 2
+RUNS = PASSES // RUN_BANKS
+RUN_PASSES = 2 * PASSES // RUNS
 UNIT_SUMS = 2 * S
 GPSIMD_SUMS = 768
 
@@ -169,17 +172,20 @@ def tile_llamaattention_pa_kernel(
                 quantise_x(r - 1)
         quantise_x(S_TILES - 1)
 
+        w_grouped_tiles = {}
         w_quantised = {}
+        acc_tiles = {}
 
-        def prepare_weights(n):
+        def turn_weights(n, run):
             w_words = raw_tiles[n][:].bitcast(F32).rearrange("p (c w) -> p c w", c=2)
-            w_grouped = grouped_pool.tile(
-                [P, UNIT_COLS * PACK], BF16, name="w_grouped", tag="w_grouped", align_bytes=64
-            )
-            w_grouped_words = w_grouped[:].bitcast(F32).rearrange(
+            if run == 0:
+                w_grouped_tiles[n] = grouped_pool.tile(
+                    [P, UNIT_COLS * PACK], BF16, name="w_grouped", tag="w_grouped", align_bytes=64
+                )
+            w_grouped_words = w_grouped_tiles[n][:].bitcast(F32).rearrange(
                 "p (g h c d u) -> p g h c d u", g=PASSES, h=2, c=2, u=2
             )
-            for g in range(PASSES):
+            for g in range(run * RUN_BANKS, (run + 1) * RUN_BANKS):
                 w_t = turn_psum.tile([P, 2, 2, P], F32, name="w_t", tag="turn")
                 for c in range(2):
                     for u in range(2):
@@ -194,6 +200,8 @@ def tile_llamaattention_pa_kernel(
                             "p c u d -> p c d u"
                         ),
                     )
+
+        def quantise_weights(n):
             w_codes = codes_pool.tile(
                 [P, UNIT_COLS], U32, name="w_codes", tag="w_codes", align_bytes=64
             )
@@ -201,28 +209,26 @@ def tile_llamaattention_pa_kernel(
                 [P, UNIT_COLS], U8, name="w_scales", tag="w_scales", align_bytes=64
             )
             nc.vector.quantize_mx(
-                out=w_codes[:].bitcast(FP8X4), scales=w_scales[:], in_=w_grouped[:]
+                out=w_codes[:].bitcast(FP8X4), scales=w_scales[:], in_=w_grouped_tiles[n][:]
             )
             w_quantised[n] = (w_codes, w_scales)
 
-        def project(n):
+        def project(n, run):
             w_codes, w_scales = w_quantised[n]
-            halves = []
-            for h in range(2):
-                acc = acc_psum.tile([P, S], F32, name="acc", tag="acc")
-                for g in range(PASSES):
-                    cols = slice((2 * g + h) * P, (2 * g + h + 1) * P)
-                    nc.tensor.matmul_mx(
-                        out=acc[:],
-                        lhsT=w_codes[:, cols].bitcast(FP8X4),
-                        lhsT_scale=w_scales[:, cols],
-                        rhs=x_codes[:, g * S : (g + 1) * S].bitcast(FP8X4),
-                        rhs_scale=x_scales[:, g * S : (g + 1) * S],
-                        start=(g == 0),
-                        stop=(g == PASSES - 1),
-                    )
-                halves.append(acc)
-            return halves
+            for i in range(run * RUN_PASSES, (run + 1) * RUN_PASSES):
+                h, g = divmod(i, PASSES)
+                if g == 0:
+                    acc_tiles[(n, h)] = acc_psum.tile([P, S], F32, name="acc", tag="acc")
+                cols = slice((2 * g + h) * P, (2 * g + h + 1) * P)
+                nc.tensor.matmul_mx(
+                    out=acc_tiles[(n, h)][:],
+                    lhsT=w_codes[:, cols].bitcast(FP8X4),
+                    lhsT_scale=w_scales[:, cols],
+                    rhs=x_codes[:, g * S : (g + 1) * S].bitcast(FP8X4),
+                    rhs_scale=x_scales[:, g * S : (g + 1) * S],
+                    start=(g == 0),
+                    stop=(g == PASSES - 1),
+                )
 
         rot_codes = []
         rot_scales = []
@@ -298,15 +304,20 @@ def tile_llamaattention_pa_kernel(
             if n % 2 == 0 and 4 <= n:
                 quantise_rot((n - 4) // 2)
 
-        prepare_weights(0)
+        for run in range(RUNS):
+            turn_weights(0, run)
+        quantise_weights(0)
         for n in range(UNITS):
             if n + LOADS_AHEAD < UNITS:
                 load_weights(n + LOADS_AHEAD)
+            for run in range(RUNS):
+                if n + 1 < UNITS:
+                    turn_weights(n + 1, run)
+                project(n, run)
             if n + 1 < UNITS:
-                prepare_weights(n + 1)
-            lo, hi = project(n)
+                quantise_weights(n + 1)
             finish_rope(n)
-            rope_products(n, lo, hi)
+            rope_products(n, acc_tiles[(n, 0)], acc_tiles[(n, 1)])
 
         mask_sb = keep.tile([P, S_TILES, S], BF16, name="mask_sb")
         nc.sync.dma_start(out=mask_sb[:], in_=mask_rows.rearrange("(m p) s -> p m s", p=P))

@@ -24,10 +24,7 @@ S_TILES = S // P
 PAIR_ROWS = 2 * HD
 UNITS = 2 * H // PAIR_ROWS
 UNIT_COLS = PASSES * 2 * P
-LOADS_AHEAD = 4
-RUN_BANKS = 2
-RUNS = PASSES // RUN_BANKS
-RUN_PASSES = 2 * PASSES // RUNS
+LOADS_AHEAD = 5
 UNIT_SUMS = 2 * S
 GPSIMD_SUMS = 768
 
@@ -176,16 +173,15 @@ def tile_llamaattention_pa_kernel(
         w_quantised = {}
         acc_tiles = {}
 
-        def turn_weights(n, run):
+        def turn_weights(n):
             w_words = raw_tiles[n][:].bitcast(F32).rearrange("p (c w) -> p c w", c=2)
-            if run == 0:
-                w_grouped_tiles[n] = grouped_pool.tile(
-                    [P, UNIT_COLS * PACK], BF16, name="w_grouped", tag="w_grouped", align_bytes=64
-                )
+            w_grouped_tiles[n] = grouped_pool.tile(
+                [P, UNIT_COLS * PACK], BF16, name="w_grouped", tag="w_grouped", align_bytes=64
+            )
             w_grouped_words = w_grouped_tiles[n][:].bitcast(F32).rearrange(
                 "p (g h c d u) -> p g h c d u", g=PASSES, h=2, c=2, u=2
             )
-            for g in range(run * RUN_BANKS, (run + 1) * RUN_BANKS):
+            for g in range(PASSES):
                 w_t = turn_psum.tile([P, 2, 2, P], F32, name="w_t", tag="turn")
                 for c in range(2):
                     for u in range(2):
@@ -213,22 +209,21 @@ def tile_llamaattention_pa_kernel(
             )
             w_quantised[n] = (w_codes, w_scales)
 
-        def project(n, run):
+        def project(n):
             w_codes, w_scales = w_quantised[n]
-            for i in range(run * RUN_PASSES, (run + 1) * RUN_PASSES):
-                h, g = divmod(i, PASSES)
-                if g == 0:
-                    acc_tiles[(n, h)] = acc_psum.tile([P, S], F32, name="acc", tag="acc")
-                cols = slice((2 * g + h) * P, (2 * g + h + 1) * P)
-                nc.tensor.matmul_mx(
-                    out=acc_tiles[(n, h)][:],
-                    lhsT=w_codes[:, cols].bitcast(FP8X4),
-                    lhsT_scale=w_scales[:, cols],
-                    rhs=x_codes[:, g * S : (g + 1) * S].bitcast(FP8X4),
-                    rhs_scale=x_scales[:, g * S : (g + 1) * S],
-                    start=(g == 0),
-                    stop=(g == PASSES - 1),
-                )
+            for h in range(2):
+                acc_tiles[(n, h)] = acc_psum.tile([P, S], F32, name="acc", tag="acc")
+                for g in range(PASSES):
+                    cols = slice((2 * g + h) * P, (2 * g + h + 1) * P)
+                    nc.tensor.matmul_mx(
+                        out=acc_tiles[(n, h)][:],
+                        lhsT=w_codes[:, cols].bitcast(FP8X4),
+                        lhsT_scale=w_scales[:, cols],
+                        rhs=x_codes[:, g * S : (g + 1) * S].bitcast(FP8X4),
+                        rhs_scale=x_scales[:, g * S : (g + 1) * S],
+                        start=(g == 0),
+                        stop=(g == PASSES - 1),
+                    )
 
         rot_codes = []
         rot_scales = []
@@ -304,16 +299,15 @@ def tile_llamaattention_pa_kernel(
             if n % 2 == 0 and 4 <= n:
                 quantise_rot((n - 4) // 2)
 
-        for run in range(RUNS):
-            turn_weights(0, run)
+        turn_weights(0)
+        turn_weights(1)
         quantise_weights(0)
         for n in range(UNITS):
             if n + LOADS_AHEAD < UNITS:
                 load_weights(n + LOADS_AHEAD)
-            for run in range(RUNS):
-                if n + 1 < UNITS:
-                    turn_weights(n + 1, run)
-                project(n, run)
+            project(n)
+            if n + 2 < UNITS:
+                turn_weights(n + 2)
             if n + 1 < UNITS:
                 quantise_weights(n + 1)
             finish_rope(n)

@@ -27,6 +27,7 @@ UNIT_COLS = PASSES * 2 * P
 LOADS_AHEAD = 5
 UNIT_SUMS = 2 * S
 GPSIMD_SUMS = 768
+FENCE_SUMS = 16
 
 COS_LO, SIN_HI, COS_HI, NEG_SIN_LO = 0, 1, 2, 3
 
@@ -259,16 +260,17 @@ def tile_llamaattention_pa_kernel(
                 rot_tiles[n // 2] = rot_pool.tile([P, PACK * S], BF16, name="rot", tag="rot")
             first = (n % 2) * UNIT_SUMS
             flat = product_tiles[n][:].rearrange("p t s -> p (t s)")
+            vector_first = GPSIMD_SUMS - FENCE_SUMS
+            nc.vector.tensor_tensor(
+                out=rot_tiles[n // 2][:, first + vector_first : first + UNIT_SUMS],
+                in0=flat[:, vector_first:UNIT_SUMS],
+                in1=flat[:, UNIT_SUMS + vector_first : 2 * UNIT_SUMS],
+                op=ADD,
+            )
             nc.gpsimd.tensor_tensor(
                 out=rot_tiles[n // 2][:, first : first + GPSIMD_SUMS],
                 in0=flat[:, 0:GPSIMD_SUMS],
                 in1=flat[:, UNIT_SUMS : UNIT_SUMS + GPSIMD_SUMS],
-                op=ADD,
-            )
-            nc.vector.tensor_tensor(
-                out=rot_tiles[n // 2][:, first + GPSIMD_SUMS : first + UNIT_SUMS],
-                in0=flat[:, GPSIMD_SUMS:UNIT_SUMS],
-                in1=flat[:, UNIT_SUMS + GPSIMD_SUMS : 2 * UNIT_SUMS],
                 op=ADD,
             )
 
@@ -292,12 +294,12 @@ def tile_llamaattention_pa_kernel(
             )
 
         def finish_rope(n):
+            if n % 2 == 0 and 4 <= n:
+                quantise_rot((n - 4) // 2)
             if 1 <= n <= UNITS:
                 rope_sums(n - 1)
             if n % 2 == 1 and 3 <= n:
                 group_rot((n - 3) // 2)
-            if n % 2 == 0 and 4 <= n:
-                quantise_rot((n - 4) // 2)
 
         turn_weights(0)
         turn_weights(1)

@@ -26,7 +26,7 @@ UNITS = 2 * H // PAIR_ROWS
 UNIT_COLS = PASSES * 2 * P
 LOADS_AHEAD = 5
 UNIT_SUMS = 2 * S
-GPSIMD_SUMS = 768
+GPSIMD_SUMS = 896
 FENCE_SUMS = 16
 
 COS_LO, SIN_HI, COS_HI, NEG_SIN_LO = 0, 1, 2, 3
@@ -89,6 +89,15 @@ def tile_llamaattention_pa_kernel(
 
         for n in range(LOADS_AHEAD):
             load_weights(n)
+
+        zeros = keep.tile([P, S], BF16, name="zeros")
+        nc.vector.memset(zeros[:], 0.0)
+
+        def keep_clock_up(pool, tag, count):
+            if count:
+                warm = pool.tile([P, S], F32, name="warm", tag=tag)
+                for repeat in range(count):
+                    nc.tensor.matmul(warm[:], lhsT=zeros[:, 0:P], rhs=zeros[:], start=True, stop=True)
 
         ident_f32 = keep.tile([P, P], F32, name="ident_f32")
         make_identity(nc, ident_f32[:])
@@ -239,21 +248,23 @@ def tile_llamaattention_pa_kernel(
         rot_tiles = {}
         rot_grouped_tiles = {}
 
-        def rope_products(n, lo, hi):
-            products = rope_pool.tile([P, 4, S], F32, name="products", tag="products")
+        def rope_products(n, lo, hi, positions=slice(0, S)):
+            if positions.start == 0:
+                product_tiles[n] = rope_pool.tile([P, 4, S], F32, name="products", tag="products")
+            products = product_tiles[n]
+            twice = [P, 2, positions.stop - positions.start]
             nc.vector.tensor_tensor(
-                out=products[:, 0:4:3, :],
-                in0=lo[:].unsqueeze(1).to_broadcast([P, 2, S]),
-                in1=tables[:, COS_LO : SIN_HI + 1, :],
+                out=products[:, 0:4:3, positions],
+                in0=lo[:, positions].unsqueeze(1).to_broadcast(twice),
+                in1=tables[:, COS_LO : SIN_HI + 1, positions],
                 op=MULT,
             )
             nc.vector.tensor_tensor(
-                out=products[:, 1:3, :],
-                in0=hi[:].unsqueeze(1).to_broadcast([P, 2, S]),
-                in1=tables[:, COS_HI : NEG_SIN_LO + 1, :],
+                out=products[:, 1:3, positions],
+                in0=hi[:, positions].unsqueeze(1).to_broadcast(twice),
+                in1=tables[:, COS_HI : NEG_SIN_LO + 1, positions],
                 op=MULT,
             )
-            product_tiles[n] = products
 
         def rope_sums(n):
             if n % 2 == 0:
@@ -293,6 +304,43 @@ def tile_llamaattention_pa_kernel(
                 in_=rot_grouped_tiles[pair][:],
             )
 
+        def finish_last_pair(half):
+            n, pair = UNITS - 1, UNITS // 2 - 1
+            positions = slice(half * (S // 2), (half + 1) * (S // 2))
+            if half == 0:
+                rot_grouped_tiles[pair] = rot_grouped_pool.tile(
+                    [P, S * PACK], BF16, name="rot_grouped", tag="rot_grouped", align_bytes=64
+                )
+            rot = rot_tiles[pair][:].rearrange("p (t s) -> p t s", t=PACK)
+            nc.vector.tensor_tensor(
+                out=rot[:, 2:4, positions],
+                in0=product_tiles[n][:, 0:2, positions],
+                in1=product_tiles[n][:, 2:4, positions],
+                op=ADD,
+            )
+
+        def group_last_pair(half, copy):
+            pair = UNITS // 2 - 1
+            positions = slice(half * (S // 2), (half + 1) * (S // 2))
+            rot = rot_tiles[pair][:].rearrange("p (t s) -> p t s", t=PACK)
+            copy(
+                out=rot_grouped_tiles[pair][
+                    :, positions.start * PACK : positions.stop * PACK
+                ].rearrange("p (c i t) -> p c t i", i=4, t=PACK),
+                in_=rot[:, :, positions].rearrange("p t (c i) -> p c t i", i=4),
+            )
+
+        def quantise_last_pair(half):
+            pair = UNITS // 2 - 1
+            first = (PASSES - 1) * S + half * (S // 2)
+            nc.vector.quantize_mx(
+                out=rot_codes[1][:, first : first + S // 2].bitcast(FP8X4),
+                scales=rot_scales[1][:, first : first + S // 2],
+                in_=rot_grouped_tiles[pair][
+                    :, half * (S // 2) * PACK : (half + 1) * (S // 2) * PACK
+                ],
+            )
+
         def finish_rope(n):
             if n % 2 == 0 and 4 <= n:
                 quantise_rot((n - 4) // 2)
@@ -313,7 +361,13 @@ def tile_llamaattention_pa_kernel(
             if n + 1 < UNITS:
                 quantise_weights(n + 1)
             finish_rope(n)
-            rope_products(n, acc_tiles[(n, 0)], acc_tiles[(n, 1)])
+            if n < UNITS - 1:
+                rope_products(n, acc_tiles[(n, 0)], acc_tiles[(n, 1)])
+
+        n = UNITS - 1
+        for half in range(2):
+            positions = slice(half * (S // 2), (half + 1) * (S // 2))
+            rope_products(n, acc_tiles[(n, 0)], acc_tiles[(n, 1)], positions)
 
         mask_sb = keep.tile([P, S_TILES, S], BF16, name="mask_sb")
         nc.sync.dma_start(out=mask_sb[:], in_=mask_rows.rearrange("(m p) s -> p m s", p=P))
@@ -322,25 +376,32 @@ def tile_llamaattention_pa_kernel(
         for m in range(S_TILES):
             scores.append(turn_psum.tile([P, S], F32, name="scores%d" % m, tag="turn"))
 
-        def add_scores(g):
+        def add_scores(g, first=0, count=S):
             for m in range(S_TILES):
                 q_cols = slice(g * S + m * P, g * S + (m + 1) * P)
-                k_cols = slice(g * S, (g + 1) * S)
+                k_cols = slice(g * S + first, g * S + first + count)
                 nc.tensor.matmul_mx(
-                    out=scores[m][:],
+                    out=scores[m][:, first : first + count],
                     lhsT=rot_codes[0][:, q_cols].bitcast(FP8X4),
                     lhsT_scale=rot_scales[0][:, q_cols],
                     rhs=rot_codes[1][:, k_cols].bitcast(FP8X4),
                     rhs_scale=rot_scales[1][:, k_cols],
                     start=(g == 0),
-                    stop=(g == PASSES - 1),
+                    stop=(g == PASSES - 1 and first + count == S),
                 )
 
         for g in range(PASSES - 1):
             add_scores(g)
-        for n in range(UNITS, UNITS + 3):
-            finish_rope(n)
-        add_scores(PASSES - 1)
+        finish_last_pair(0)
+        finish_last_pair(1)
+        quantise_rot(UNITS // 2 - 2)
+        group_last_pair(0, nc.scalar.copy)
+        group_last_pair(1, nc.vector.tensor_copy)
+        quantise_last_pair(0)
+        quantise_last_pair(1)
+        keep_clock_up(acc_psum, "acc", 8)
+        add_scores(PASSES - 1, 0, S // 2)
+        add_scores(PASSES - 1, S // 2, S // 2)
 
         for m in range(S_TILES):
             result = out_pool.tile([P, S], F32, name="result", tag="result")

@@ -58,20 +58,7 @@ def tile_llamaattention_pa_kernel(
 
         cos_sb = keep.tile([P, S_TILES * HD], BF16, name="cos_sb")
         sin_sb = keep.tile([P, S_TILES * HD], BF16, name="sin_sb")
-        nc.scalar.dma_start(
-            out=cos_sb[:].rearrange("p (r d) -> p r d", r=S_TILES),
-            in_=cos.rearrange("(r p) d -> p r d", p=P),
-        )
-        nc.scalar.dma_start(
-            out=sin_sb[:].rearrange("p (r d) -> p r d", r=S_TILES),
-            in_=sin.rearrange("(r p) d -> p r d", p=P),
-        )
-
         x_raw = keep.tile([P, S_TILES * H], BF16, name="x_raw")
-        for r in range(S_TILES):
-            nc.sync.dma_start(
-                out=x_raw[:, r * H : (r + 1) * H], in_=x_rows[r * P : (r + 1) * P, :]
-            )
 
         raw_tiles = {}
 
@@ -87,17 +74,30 @@ def tile_llamaattention_pa_kernel(
             )
             raw_tiles[n] = w_raw
 
-        for n in range(LOADS_AHEAD):
+        load_weights(0)
+        nc.sync.dma_start(
+            out=cos_sb[:].rearrange("p (r d) -> p r d", r=S_TILES),
+            in_=cos.rearrange("(r p) d -> p r d", p=P),
+        )
+        nc.sync.dma_start(
+            out=sin_sb[:].rearrange("p (r d) -> p r d", r=S_TILES),
+            in_=sin.rearrange("(r p) d -> p r d", p=P),
+        )
+        for r in range(0, 4):
+            nc.sync.dma_start(
+                out=x_raw[:, r * H : (r + 1) * H], in_=x_rows[r * P : (r + 1) * P, :]
+            )
+        load_weights(1)
+        for n in range(2, LOADS_AHEAD):
             load_weights(n)
 
         zeros = keep.tile([P, S], BF16, name="zeros")
         nc.vector.memset(zeros[:], 0.0)
 
         def keep_clock_up(pool, tag, count):
-            if count:
-                warm = pool.tile([P, S], F32, name="warm", tag=tag)
-                for repeat in range(count):
-                    nc.tensor.matmul(warm[:], lhsT=zeros[:, 0:P], rhs=zeros[:], start=True, stop=True)
+            warm = pool.tile([P, S], F32, name="warm", tag=tag)
+            for repeat in range(count):
+                nc.tensor.matmul(warm[:], lhsT=zeros[:, 0:P], rhs=zeros[:], start=True, stop=True)
 
         ident_f32 = keep.tile([P, P], F32, name="ident_f32")
         make_identity(nc, ident_f32[:])
@@ -130,7 +130,8 @@ def tile_llamaattention_pa_kernel(
         )
         doubled_tiles = doubled[:].rearrange("p (r t f) -> p r t f", r=S_TILES, t=4)
         tables = keep.tile([P, 4, S], BF16, name="tables")
-        for b in range(2):
+
+        def turn_tables(b, copy):
             tables_t = acc_psum.tile([P, 2, S], BF16, name="tables_t", tag="acc")
             for t in range(2):
                 for r in range(S_TILES):
@@ -139,7 +140,7 @@ def tile_llamaattention_pa_kernel(
                         doubled_tiles[:, r, 2 * b + t, :],
                         ident_bf16[:],
                     )
-            nc.scalar.copy(out=tables[:, 2 * b : 2 * b + 2, :], in_=tables_t[:])
+            copy(out=tables[:, 2 * b : 2 * b + 2, :], in_=tables_t[:])
 
         x_words = x_raw[:].bitcast(F32).rearrange("p (r w) -> p r w", r=S_TILES)
         x_grouped = keep.tile([P, PASSES * S * PACK], BF16, name="x_grouped", align_bytes=64)
@@ -149,7 +150,7 @@ def tile_llamaattention_pa_kernel(
         x_codes = keep.tile([P, PASSES * S], U32, name="x_codes", align_bytes=64)
         x_scales = keep.tile([P, PASSES * S], U8, name="x_scales", align_bytes=64)
 
-        def turn_x(r):
+        def turn_x(r, copies):
             for half in range(2):
                 x_t = acc_psum.tile([P, 2, 2, P], F32, name="x_t", tag="acc")
                 for g in range(2):
@@ -158,8 +159,7 @@ def tile_llamaattention_pa_kernel(
                         nc.tensor.transpose(
                             x_t[:, g, u, :], x_words[:, r, block : block + P], ident_f32[:]
                         )
-                copy = nc.scalar.copy if half == 0 else nc.vector.tensor_copy
-                copy(
+                copies[half](
                     out=x_grouped_words[:, 2 * half : 2 * half + 2, r * P : (r + 1) * P, :],
                     in_=x_t[:].rearrange("p g u s -> p g s u"),
                 )
@@ -173,17 +173,11 @@ def tile_llamaattention_pa_kernel(
                     in_=x_grouped[:, first * PACK : (first + P) * PACK],
                 )
 
-        for r in range(S_TILES):
-            turn_x(r)
-            if r > 0:
-                quantise_x(r - 1)
-        quantise_x(S_TILES - 1)
-
         w_grouped_tiles = {}
         w_quantised = {}
         acc_tiles = {}
 
-        def turn_weights(n):
+        def turn_weights(n, copies=None):
             w_words = raw_tiles[n][:].bitcast(F32).rearrange("p (c w) -> p c w", c=2)
             w_grouped_tiles[n] = grouped_pool.tile(
                 [P, UNIT_COLS * PACK], BF16, name="w_grouped", tag="w_grouped", align_bytes=64
@@ -199,8 +193,9 @@ def tile_llamaattention_pa_kernel(
                         nc.tensor.transpose(
                             w_t[:, c, u, :], w_words[:, c, block : block + P], ident_f32[:]
                         )
+                copy = copies[g % 2] if copies else nc.scalar.copy
                 for h in range(2):
-                    nc.scalar.copy(
+                    copy(
                         out=w_grouped_words[:, g, h, :, :, :],
                         in_=w_t[:, :, :, h * HALF : (h + 1) * HALF].rearrange(
                             "p c u d -> p c d u"
@@ -219,18 +214,20 @@ def tile_llamaattention_pa_kernel(
             )
             w_quantised[n] = (w_codes, w_scales)
 
-        def project(n):
+        def project(n, first=0, count=S, halves=(0, 1)):
             w_codes, w_scales = w_quantised[n]
-            for h in range(2):
-                acc_tiles[(n, h)] = acc_psum.tile([P, S], F32, name="acc", tag="acc")
+            for h in halves:
+                if first == 0:
+                    acc_tiles[(n, h)] = acc_psum.tile([P, S], F32, name="acc", tag="acc")
                 for g in range(PASSES):
                     cols = slice((2 * g + h) * P, (2 * g + h + 1) * P)
+                    x_cols = slice(g * S + first, g * S + first + count)
                     nc.tensor.matmul_mx(
-                        out=acc_tiles[(n, h)][:],
+                        out=acc_tiles[(n, h)][:, first : first + count],
                         lhsT=w_codes[:, cols].bitcast(FP8X4),
                         lhsT_scale=w_scales[:, cols],
-                        rhs=x_codes[:, g * S : (g + 1) * S].bitcast(FP8X4),
-                        rhs_scale=x_scales[:, g * S : (g + 1) * S],
+                        rhs=x_codes[:, x_cols].bitcast(FP8X4),
+                        rhs_scale=x_scales[:, x_cols],
                         start=(g == 0),
                         stop=(g == PASSES - 1),
                     )
@@ -342,27 +339,45 @@ def tile_llamaattention_pa_kernel(
             )
 
         def finish_rope(n):
-            if n % 2 == 0 and 4 <= n:
-                quantise_rot((n - 4) // 2)
             if 1 <= n <= UNITS:
                 rope_sums(n - 1)
             if n % 2 == 1 and 3 <= n:
                 group_rot((n - 3) // 2)
 
-        turn_weights(0)
-        turn_weights(1)
+        keep_clock_up(turn_psum, "turn", 8)
+        turn_weights(0, (nc.scalar.copy, nc.vector.tensor_copy))
+        keep_clock_up(turn_psum, "turn", 2)
+        turn_x(0, (nc.scalar.copy, nc.scalar.copy))
+        keep_clock_up(turn_psum, "turn", 2)
+        turn_x(1, (nc.scalar.copy, nc.scalar.copy))
         quantise_weights(0)
+        turn_tables(0, nc.vector.tensor_copy)
+        quantise_x(0)
+        keep_clock_up(turn_psum, "turn", 2)
+        turn_x(2, (nc.scalar.copy, nc.scalar.copy))
+        quantise_x(1)
+        turn_tables(1, nc.vector.tensor_copy)
+        keep_clock_up(turn_psum, "turn", 2)
+        turn_x(3, (nc.scalar.copy, nc.vector.tensor_copy))
+        quantise_x(2)
+        quantise_x(3)
+        keep_clock_up(turn_psum, "turn", 2)
+        turn_weights(1)
+        project(0)
         for n in range(UNITS):
             if n + LOADS_AHEAD < UNITS:
                 load_weights(n + LOADS_AHEAD)
-            project(n)
-            if n + 2 < UNITS:
+            if n > 0:
+                project(n)
+            if 1 < n + 2 < UNITS:
                 turn_weights(n + 2)
-            if n + 1 < UNITS:
+            if 0 < n + 1 < UNITS:
                 quantise_weights(n + 1)
             finish_rope(n)
             if n < UNITS - 1:
                 rope_products(n, acc_tiles[(n, 0)], acc_tiles[(n, 1)])
+            if n % 2 == 0 and 4 <= n:
+                quantise_rot((n - 4) // 2)
 
         n = UNITS - 1
         for half in range(2):
@@ -376,18 +391,18 @@ def tile_llamaattention_pa_kernel(
         for m in range(S_TILES):
             scores.append(turn_psum.tile([P, S], F32, name="scores%d" % m, tag="turn"))
 
-        def add_scores(g, first=0, count=S):
+        def add_scores(g):
             for m in range(S_TILES):
                 q_cols = slice(g * S + m * P, g * S + (m + 1) * P)
-                k_cols = slice(g * S + first, g * S + first + count)
+                k_cols = slice(g * S, (g + 1) * S)
                 nc.tensor.matmul_mx(
-                    out=scores[m][:, first : first + count],
+                    out=scores[m][:],
                     lhsT=rot_codes[0][:, q_cols].bitcast(FP8X4),
                     lhsT_scale=rot_scales[0][:, q_cols],
                     rhs=rot_codes[1][:, k_cols].bitcast(FP8X4),
                     rhs_scale=rot_scales[1][:, k_cols],
                     start=(g == 0),
-                    stop=(g == PASSES - 1 and first + count == S),
+                    stop=(g == PASSES - 1),
                 )
 
         for g in range(PASSES - 1):
@@ -399,9 +414,7 @@ def tile_llamaattention_pa_kernel(
         group_last_pair(1, nc.vector.tensor_copy)
         quantise_last_pair(0)
         quantise_last_pair(1)
-        keep_clock_up(acc_psum, "acc", 8)
-        add_scores(PASSES - 1, 0, S // 2)
-        add_scores(PASSES - 1, S // 2, S // 2)
+        add_scores(PASSES - 1)
 
         for m in range(S_TILES):
             result = out_pool.tile([P, S], F32, name="result", tag="result")

@@ -74,7 +74,6 @@ def tile_llamaattention_pa_kernel(
             )
             raw_tiles[n] = w_raw
 
-        load_weights(0)
         nc.sync.dma_start(
             out=cos_sb[:].rearrange("p (r d) -> p r d", r=S_TILES),
             in_=cos.rearrange("(r p) d -> p r d", p=P),
@@ -83,6 +82,7 @@ def tile_llamaattention_pa_kernel(
             out=sin_sb[:].rearrange("p (r d) -> p r d", r=S_TILES),
             in_=sin.rearrange("(r p) d -> p r d", p=P),
         )
+        load_weights(0)
         for r in range(0, 4):
             nc.sync.dma_start(
                 out=x_raw[:, r * H : (r + 1) * H], in_=x_rows[r * P : (r + 1) * P, :]
@@ -95,9 +95,10 @@ def tile_llamaattention_pa_kernel(
         nc.vector.memset(zeros[:], 0.0)
 
         def keep_clock_up(pool, tag, count):
-            warm = pool.tile([P, S], F32, name="warm", tag=tag)
-            for repeat in range(count):
-                nc.tensor.matmul(warm[:], lhsT=zeros[:, 0:P], rhs=zeros[:], start=True, stop=True)
+            if count:
+                warm = pool.tile([P, S], F32, name="warm", tag=tag)
+                for repeat in range(count):
+                    nc.tensor.matmul(warm[:], lhsT=zeros[:, 0:P], rhs=zeros[:], start=True, stop=True)
 
         ident_f32 = keep.tile([P, P], F32, name="ident_f32")
         make_identity(nc, ident_f32[:])
@@ -269,16 +270,20 @@ def tile_llamaattention_pa_kernel(
             first = (n % 2) * UNIT_SUMS
             flat = product_tiles[n][:].rearrange("p t s -> p (t s)")
             vector_first = GPSIMD_SUMS - FENCE_SUMS
-            nc.vector.tensor_tensor(
-                out=rot_tiles[n // 2][:, first + vector_first : first + UNIT_SUMS],
-                in0=flat[:, vector_first:UNIT_SUMS],
-                in1=flat[:, UNIT_SUMS + vector_first : 2 * UNIT_SUMS],
-                op=ADD,
-            )
+            gpsimd_end = GPSIMD_SUMS
+            if n == UNITS - 2:
+                gpsimd_end = UNIT_SUMS
+            else:
+                nc.vector.tensor_tensor(
+                    out=rot_tiles[n // 2][:, first + vector_first : first + UNIT_SUMS],
+                    in0=flat[:, vector_first:UNIT_SUMS],
+                    in1=flat[:, UNIT_SUMS + vector_first : 2 * UNIT_SUMS],
+                    op=ADD,
+                )
             nc.gpsimd.tensor_tensor(
-                out=rot_tiles[n // 2][:, first : first + GPSIMD_SUMS],
-                in0=flat[:, 0:GPSIMD_SUMS],
-                in1=flat[:, UNIT_SUMS : UNIT_SUMS + GPSIMD_SUMS],
+                out=rot_tiles[n // 2][:, first : first + gpsimd_end],
+                in0=flat[:, 0:gpsimd_end],
+                in1=flat[:, UNIT_SUMS : UNIT_SUMS + gpsimd_end],
                 op=ADD,
             )
 
@@ -344,24 +349,23 @@ def tile_llamaattention_pa_kernel(
             if n % 2 == 1 and 3 <= n:
                 group_rot((n - 3) // 2)
 
-        keep_clock_up(turn_psum, "turn", 8)
-        turn_weights(0, (nc.scalar.copy, nc.vector.tensor_copy))
-        keep_clock_up(turn_psum, "turn", 2)
-        turn_x(0, (nc.scalar.copy, nc.scalar.copy))
-        keep_clock_up(turn_psum, "turn", 2)
-        turn_x(1, (nc.scalar.copy, nc.scalar.copy))
-        quantise_weights(0)
+        keep_clock_up(acc_psum, "acc", 7)
         turn_tables(0, nc.vector.tensor_copy)
+        turn_tables(1, nc.scalar.copy)
+        keep_clock_up(acc_psum, "acc", 2)
+        turn_weights(0, (nc.scalar.copy, nc.vector.tensor_copy))
+        keep_clock_up(acc_psum, "acc", 2)
+        turn_x(0, (nc.scalar.copy, nc.scalar.copy))
+        turn_x(1, (nc.scalar.copy, nc.scalar.copy))
+        keep_clock_up(acc_psum, "acc", 2)
+        quantise_weights(0)
         quantise_x(0)
-        keep_clock_up(turn_psum, "turn", 2)
         turn_x(2, (nc.scalar.copy, nc.scalar.copy))
         quantise_x(1)
-        turn_tables(1, nc.vector.tensor_copy)
-        keep_clock_up(turn_psum, "turn", 2)
         turn_x(3, (nc.scalar.copy, nc.vector.tensor_copy))
+        keep_clock_up(acc_psum, "acc", 2)
         quantise_x(2)
         quantise_x(3)
-        keep_clock_up(turn_psum, "turn", 2)
         turn_weights(1)
         project(0)
         for n in range(UNITS):

@@ -25,9 +25,8 @@ PAIR_ROWS = 2 * HD
 UNITS = 2 * H // PAIR_ROWS
 UNIT_COLS = PASSES * 2 * P
 LOADS_AHEAD = 5
-UNIT_SUMS = 2 * S
-GPSIMD_SUMS = 896
-FENCE_SUMS = 16
+GPSIMD_POSITIONS = 448
+FENCE = 8
 
 COS_LO, SIN_HI, COS_HI, NEG_SIN_LO = 0, 1, 2, 3
 
@@ -264,83 +263,46 @@ def tile_llamaattention_pa_kernel(
                 op=MULT,
             )
 
+        def add_products(engine, n, first, end):
+            out = rot_tiles[n // 2][:].rearrange("p (j s h) -> p j s h", j=2, h=2)[
+                :, n % 2, first:end, :
+            ]
+            runs = product_tiles[n][:, :, first:end].rearrange("p t (c i) -> p c t i", i=4)
+            engine.tensor_tensor(
+                out=out.rearrange("p (c i) h -> p c h i", i=4),
+                in0=runs[:, :, 0:2, :],
+                in1=runs[:, :, 2:4, :],
+                op=ADD,
+            )
+
         def rope_sums(n):
             if n % 2 == 0:
                 rot_tiles[n // 2] = rot_pool.tile([P, PACK * S], BF16, name="rot", tag="rot")
-            first = (n % 2) * UNIT_SUMS
-            flat = product_tiles[n][:].rearrange("p t s -> p (t s)")
-            vector_first = GPSIMD_SUMS - FENCE_SUMS
-            gpsimd_end = GPSIMD_SUMS
             if n == UNITS - 2:
-                gpsimd_end = UNIT_SUMS
-            else:
-                nc.vector.tensor_tensor(
-                    out=rot_tiles[n // 2][:, first + vector_first : first + UNIT_SUMS],
-                    in0=flat[:, vector_first:UNIT_SUMS],
-                    in1=flat[:, UNIT_SUMS + vector_first : 2 * UNIT_SUMS],
-                    op=ADD,
-                )
-            nc.gpsimd.tensor_tensor(
-                out=rot_tiles[n // 2][:, first : first + gpsimd_end],
-                in0=flat[:, 0:gpsimd_end],
-                in1=flat[:, UNIT_SUMS : UNIT_SUMS + gpsimd_end],
-                op=ADD,
-            )
+                add_products(nc.gpsimd, n, 0, S)
+                return
+            add_products(nc.vector, n, GPSIMD_POSITIONS - FENCE, S)
+            add_products(nc.gpsimd, n, 0, GPSIMD_POSITIONS)
 
-        def group_rot(pair):
-            rot_grouped = rot_grouped_pool.tile(
-                [P, S * PACK], BF16, name="rot_grouped", tag="rot_grouped", align_bytes=64
-            )
-            nc.scalar.copy(
-                out=rot_grouped[:].rearrange("p (c i t) -> p c t i", i=4, t=PACK),
-                in_=rot_tiles[pair][:].rearrange("p (t c i) -> p c t i", t=PACK, i=4),
-            )
-            rot_grouped_tiles[pair] = rot_grouped
-
-        def quantise_rot(pair):
-            which = pair % 2
-            cols = slice((pair // 2) * S, (pair // 2 + 1) * S)
-            nc.vector.quantize_mx(
-                out=rot_codes[which][:, cols].bitcast(FP8X4),
-                scales=rot_scales[which][:, cols],
-                in_=rot_grouped_tiles[pair][:],
-            )
-
-        def finish_last_pair(half):
-            n, pair = UNITS - 1, UNITS // 2 - 1
-            positions = slice(half * (S // 2), (half + 1) * (S // 2))
-            if half == 0:
+        def group_rot(pair, copy=nc.scalar.copy, first=0, count=S):
+            if first == 0:
                 rot_grouped_tiles[pair] = rot_grouped_pool.tile(
                     [P, S * PACK], BF16, name="rot_grouped", tag="rot_grouped", align_bytes=64
                 )
-            rot = rot_tiles[pair][:].rearrange("p (t s) -> p t s", t=PACK)
-            nc.vector.tensor_tensor(
-                out=rot[:, 2:4, positions],
-                in0=product_tiles[n][:, 0:2, positions],
-                in1=product_tiles[n][:, 2:4, positions],
-                op=ADD,
-            )
-
-        def group_last_pair(half, copy):
-            pair = UNITS // 2 - 1
-            positions = slice(half * (S // 2), (half + 1) * (S // 2))
-            rot = rot_tiles[pair][:].rearrange("p (t s) -> p t s", t=PACK)
+            words = rot_tiles[pair][:].bitcast(F32).rearrange("p (j s) -> p j s", j=2)
+            grouped = rot_grouped_tiles[pair][:].bitcast(F32).rearrange("p (s j) -> p s j", j=2)
             copy(
-                out=rot_grouped_tiles[pair][
-                    :, positions.start * PACK : positions.stop * PACK
-                ].rearrange("p (c i t) -> p c t i", i=4, t=PACK),
-                in_=rot[:, :, positions].rearrange("p t (c i) -> p c t i", i=4),
+                out=grouped[:, first : first + count, :],
+                in_=words[:, :, first : first + count].rearrange("p j s -> p s j"),
             )
 
-        def quantise_last_pair(half):
-            pair = UNITS // 2 - 1
-            first = (PASSES - 1) * S + half * (S // 2)
+        def quantise_rot(pair, first=0, count=S):
+            which = pair % 2
+            cols = slice((pair // 2) * S + first, (pair // 2) * S + first + count)
             nc.vector.quantize_mx(
-                out=rot_codes[1][:, first : first + S // 2].bitcast(FP8X4),
-                scales=rot_scales[1][:, first : first + S // 2],
-                in_=rot_grouped_tiles[pair][
-                    :, half * (S // 2) * PACK : (half + 1) * (S // 2) * PACK
-                ],
+                out=rot_codes[which][:, cols].bitcast(FP8X4),
+                scales=rot_scales[which][:, cols],
+                in_=rot_grouped_tiles[pair][:, first * PACK : (first + count) * PACK],
             )
 
         def finish_rope(n):
@@ -411,13 +373,14 @@ def tile_llamaattention_pa_kernel(
 
         for g in range(PASSES - 1):
             add_scores(g)
-        finish_last_pair(0)
-        finish_last_pair(1)
+        half = S // 2
+        add_products(nc.vector, UNITS - 1, 0, half)
+        add_products(nc.vector, UNITS - 1, half, S)
         quantise_rot(UNITS // 2 - 2)
-        group_last_pair(0, nc.scalar.copy)
-        group_last_pair(1, nc.vector.tensor_copy)
-        quantise_last_pair(0)
-        quantise_last_pair(1)
+        group_rot(UNITS // 2 - 1, nc.scalar.copy, 0, half)
+        group_rot(UNITS // 2 - 1, nc.vector.tensor_copy, half, half)
+        quantise_rot(UNITS // 2 - 1, 0, half)
+        quantise_rot(UNITS // 2 - 1, half, half)
         add_scores(PASSES - 1)
 
         for m in range(S_TILES):

@@ -209,9 +209,13 @@ def tile_llamaattention_pa_kernel(
             w_scales = codes_pool.tile(
                 [P, UNIT_COLS], U8, name="w_scales", tag="w_scales", align_bytes=64
             )
-            nc.vector.quantize_mx(
-                out=w_codes[:].bitcast(FP8X4), scales=w_scales[:], in_=w_grouped_tiles[n][:]
-            )
+            for part in range(2):
+                cols = slice(part * UNIT_COLS // 2, (part + 1) * UNIT_COLS // 2)
+                nc.vector.quantize_mx(
+                    out=w_codes[:, cols].bitcast(FP8X4),
+                    scales=w_scales[:, cols],
+                    in_=w_grouped_tiles[n][:, cols.start * PACK : cols.stop * PACK],
+                )
             w_quantised[n] = (w_codes, w_scales)
 
         def project(n, first=0, count=S, halves=(0, 1)):
@@ -353,16 +357,17 @@ def tile_llamaattention_pa_kernel(
         mask_sb = keep.tile([P, S_TILES, S], BF16, name="mask_sb")
         nc.sync.dma_start(out=mask_sb[:], in_=mask_rows.rearrange("(m p) s -> p m s", p=P))
 
-        scores = []
-        for m in range(S_TILES):
-            scores.append(turn_psum.tile([P, S], F32, name="scores%d" % m, tag="turn"))
+        scores = {}
 
-        def add_scores(g):
+        def add_scores(g, half):
             for m in range(S_TILES):
+                if g == 0:
+                    pool, tag = ((turn_psum, "turn"), (acc_psum, "acc"))[half]
+                    scores[(m, half)] = pool.tile([P, S // 2], F32, name="scores", tag=tag)
                 q_cols = slice(g * S + m * P, g * S + (m + 1) * P)
-                k_cols = slice(g * S, (g + 1) * S)
+                k_cols = slice(g * S + half * (S // 2), g * S + (half + 1) * (S // 2))
                 nc.tensor.matmul_mx(
-                    out=scores[m][:],
+                    out=scores[(m, half)][:],
                     lhsT=rot_codes[0][:, q_cols].bitcast(FP8X4),
                     lhsT_scale=rot_scales[0][:, q_cols],
                     rhs=rot_codes[1][:, k_cols].bitcast(FP8X4),
@@ -371,26 +376,33 @@ def tile_llamaattention_pa_kernel(
                     stop=(g == PASSES - 1),
                 )
 
-        for g in range(PASSES - 1):
-            add_scores(g)
+        for h in range(2):
+            for g in range(PASSES - 1):
+                add_scores(g, h)
         half = S // 2
         add_products(nc.vector, UNITS - 1, 0, half)
         add_products(nc.vector, UNITS - 1, half, S)
         quantise_rot(UNITS // 2 - 2)
         group_rot(UNITS // 2 - 1, nc.scalar.copy, 0, half)
-        group_rot(UNITS // 2 - 1, nc.vector.tensor_copy, half, half)
+        group_rot(UNITS // 2 - 1, nc.scalar.copy, half, half)
         quantise_rot(UNITS // 2 - 1, 0, half)
         quantise_rot(UNITS // 2 - 1, half, half)
-        add_scores(PASSES - 1)
-
-        for m in range(S_TILES):
-            result = out_pool.tile([P, S], F32, name="result", tag="result")
-            nc.vector.scalar_tensor_tensor(
-                out=result[:],
-                in0=scores[m][:],
-                scalar=1.0 / math.sqrt(HD),
-                in1=mask_sb[:, m, :],
-                op0=MULT,
-                op1=ADD,
-            )
-            nc.sync.dma_start(out=out_rows[m * P : (m + 1) * P, :], in_=result[:])
+        for h in range(2):
+            add_scores(PASSES - 1, h)
+        results = []
+        for h in range(2):
+            for m in range(S_TILES):
+                if h == 0:
+                    results.append(out_pool.tile([P, S], F32, name="result", tag="result"))
+                cols = slice(h * half, (h + 1) * half)
+                nc.vector.scalar_tensor_tensor(
+                    out=results[m][:, cols],
+                    in0=scores[(m, h)][:],
+                    scalar=1.0 / math.sqrt(HD),
+                    in1=mask_sb[:, m, cols],
+                    op0=MULT,
+                    op1=ADD,
+                )
+                nc.sync.dma_start(
+                    out=out_rows[m * P : (m + 1) * P, cols], in_=results[m][:, cols]
+                )

import math
from contextlib import ExitStack

import concourse.mybir as mybir
from concourse.masks import make_identity

BF16 = mybir.dt.bfloat16
F32 = mybir.dt.float32
U32 = mybir.dt.uint32
U8 = mybir.dt.uint8
FP8X4 = mybir.dt.float8_e4m3fn_x4
MULT = mybir.AluOpType.mult
ADD = mybir.AluOpType.add

P = 128
S = 512
H = 2048
HD = 128
HALF = HD // 2
PACK = 4
K_PASS = P * PACK
PASSES = H // K_PASS
S_TILES = S // P
PAIR_ROWS = 2 * HD
UNITS = 2 * H // PAIR_ROWS
UNIT_COLS = PASSES * 2 * P
LOADS_AHEAD = 5
GPSIMD_POSITIONS = 448
FENCE = 8

COS_LO, SIN_HI, COS_HI, NEG_SIN_LO = 0, 1, 2, 3

FLOPS = 2 * (2 * S * H * H) + 2 * S * S * H


def tile_llamaattention_pa_kernel(
    tc, hidden_states, wq_deq, wk_deq, cos, sin, attention_mask, out
):
    nc = tc.nc
    x_rows = hidden_states.flatten_outer_dims()
    mask_rows = attention_mask.flatten_outer_dims()
    out_rows = out.flatten_outer_dims()
    weights = (wq_deq, wk_deq)

    with ExitStack() as ctx:
        keep = ctx.enter_context(tc.tile_pool(name="keep", bufs=1))
        raw_pool = ctx.enter_context(tc.tile_pool(name="raw", bufs=LOADS_AHEAD))
        grouped_pool = ctx.enter_context(tc.tile_pool(name="grouped", bufs=2))
        codes_pool = ctx.enter_context(tc.tile_pool(name="codes", bufs=2))
        rope_pool = ctx.enter_context(tc.tile_pool(name="rope", bufs=3))
        rot_pool = ctx.enter_context(tc.tile_pool(name="rot", bufs=3))
        rot_grouped_pool = ctx.enter_context(tc.tile_pool(name="rotg", bufs=2))
        out_pool = ctx.enter_context(tc.tile_pool(name="outp", bufs=S_TILES))
        turn_psum = ctx.enter_context(tc.psum_pool(name="turn", bufs=4))
        acc_psum = ctx.enter_context(tc.psum_pool(name="acc", bufs=4))
        ctx.enter_context(tc.manual_schedule())

        cos_sb = keep.tile([P, S_TILES * HD], BF16, name="cos_sb")
        sin_sb = keep.tile([P, S_TILES * HD], BF16, name="sin_sb")
        x_raw = keep.tile([P, S_TILES * H], BF16, name="x_raw")

        raw_tiles = {}

        def load_weights(n):
            which = (n % 4) // 2
            row0 = (2 * (n // 4) + n % 2) * PAIR_ROWS
            w_raw = raw_pool.tile([P, 2 * H], BF16, name="w_raw", tag="w_raw")
            nc.sync.dma_start(
                out=w_raw[:].rearrange("p (c k) -> p c k", c=2),
                in_=weights[which][row0 : row0 + PAIR_ROWS, :].rearrange(
                    "(c p) k -> p c k", p=P
                ),
            )
            raw_tiles[n] = w_raw

        nc.sync.dma_start(
            out=cos_sb[:].rearrange("p (r d) -> p r d", r=S_TILES),
            in_=cos.rearrange("(r p) d -> p r d", p=P),
        )
        nc.sync.dma_start(
            out=sin_sb[:].rearrange("p (r d) -> p r d", r=S_TILES),
            in_=sin.rearrange("(r p) d -> p r d", p=P),
        )
        load_weights(0)
        for r in range(0, 4):
            nc.sync.dma_start(
                out=x_raw[:, r * H : (r + 1) * H], in_=x_rows[r * P : (r + 1) * P, :]
            )
        load_weights(1)
        for n in range(2, LOADS_AHEAD):
            load_weights(n)

        zeros = keep.tile([P, S], BF16, name="zeros")
        nc.vector.memset(zeros[:], 0.0)

        def keep_clock_up(pool, tag, count):
            if count:
                warm = pool.tile([P, S], F32, name="warm", tag=tag)
                for repeat in range(count):
                    nc.tensor.matmul(warm[:], lhsT=zeros[:, 0:P], rhs=zeros[:], start=True, stop=True)

        ident_f32 = keep.tile([P, P], F32, name="ident_f32")
        make_identity(nc, ident_f32[:])
        ident_bf16 = keep.tile([P, P], BF16, name="ident_bf16")
        make_identity(nc, ident_bf16[:])

        doubled = keep.tile([P, S_TILES * 4 * P], BF16, name="doubled")
        doubled_halves = doubled[:].rearrange(
            "p (r t c d) -> p r t c d", r=S_TILES, t=4, c=2
        )
        cos_halves = cos_sb[:].rearrange("p (r h d) -> p r h d", r=S_TILES, h=2)
        sin_halves = sin_sb[:].rearrange("p (r h d) -> p r h d", r=S_TILES, h=2)
        twice = [P, S_TILES, 2, HALF]
        nc.vector.tensor_copy(
            out=doubled_halves[:, :, COS_LO, :, :],
            in_=cos_halves[:, :, 0, :].unsqueeze(2).to_broadcast(twice),
        )
        nc.vector.tensor_copy(
            out=doubled_halves[:, :, SIN_HI, :, :],
            in_=sin_halves[:, :, 1, :].unsqueeze(2).to_broadcast(twice),
        )
        nc.vector.tensor_copy(
            out=doubled_halves[:, :, COS_HI, :, :],
            in_=cos_halves[:, :, 1, :].unsqueeze(2).to_broadcast(twice),
        )
        nc.vector.tensor_scalar_mul(
            out=doubled_halves[:, :, NEG_SIN_LO, :, :],
            in0=sin_halves[:, :, 0, :].unsqueeze(2).to_broadcast(twice),
            scalar1=-1.0,
        )
        doubled_tiles = doubled[:].rearrange("p (r t f) -> p r t f", r=S_TILES, t=4)
        tables = keep.tile([P, 4, S], BF16, name="tables")

        def turn_tables(b, copy):
            tables_t = acc_psum.tile([P, 2, S], BF16, name="tables_t", tag="acc")
            for t in range(2):
                for r in range(S_TILES):
                    nc.tensor.transpose(
                        tables_t[:, t, r * P : (r + 1) * P],
                        doubled_tiles[:, r, 2 * b + t, :],
                        ident_bf16[:],
                    )
            copy(out=tables[:, 2 * b : 2 * b + 2, :], in_=tables_t[:])

        x_words = x_raw[:].bitcast(F32).rearrange("p (r w) -> p r w", r=S_TILES)
        x_grouped = keep.tile([P, PASSES * S * PACK], BF16, name="x_grouped", align_bytes=64)
        x_grouped_words = x_grouped[:].bitcast(F32).rearrange(
            "p (g s u) -> p g s u", g=PASSES, u=2
        )
        x_codes = keep.tile([P, PASSES * S], U32, name="x_codes", align_bytes=64)
        x_scales = keep.tile([P, PASSES * S], U8, name="x_scales", align_bytes=64)

        def turn_x(r, copies):
            for half in range(2):
                x_t = acc_psum.tile([P, 2, 2, P], F32, name="x_t", tag="acc")
                for g in range(2):
                    for u in range(2):
                        block = (2 * (2 * half + g) + u) * P
                        nc.tensor.transpose(
                            x_t[:, g, u, :], x_words[:, r, block : block + P], ident_f32[:]
                        )
                copies[half](
                    out=x_grouped_words[:, 2 * half : 2 * half + 2, r * P : (r + 1) * P, :],
                    in_=x_t[:].rearrange("p g u s -> p g s u"),
                )

        def quantise_x(r):
            for g in range(PASSES):
                first = g * S + r * P
                nc.vector.quantize_mx(
                    out=x_codes[:, first : first + P].bitcast(FP8X4),
                    scales=x_scales[:, first : first + P],
                    in_=x_grouped[:, first * PACK : (first + P) * PACK],
                )

        w_grouped_tiles = {}
        w_quantised = {}
        acc_tiles = {}

        def turn_weights(n, copies=None):
            w_words = raw_tiles[n][:].bitcast(F32).rearrange("p (c w) -> p c w", c=2)
            w_grouped_tiles[n] = grouped_pool.tile(
                [P, UNIT_COLS * PACK], BF16, name="w_grouped", tag="w_grouped", align_bytes=64
            )
            w_grouped_words = w_grouped_tiles[n][:].bitcast(F32).rearrange(
                "p (g h c d u) -> p g h c d u", g=PASSES, h=2, c=2, u=2
            )
            for g in range(PASSES):
                w_t = turn_psum.tile([P, 2, 2, P], F32, name="w_t", tag="turn")
                for c in range(2):
                    for u in range(2):
                        block = (2 * g + u) * P
                        nc.tensor.transpose(
                            w_t[:, c, u, :], w_words[:, c, block : block + P], ident_f32[:]
                        )
                copy = copies[g % 2] if copies else nc.scalar.copy
                for h in range(2):
                    copy(
                        out=w_grouped_words[:, g, h, :, :, :],
                        in_=w_t[:, :, :, h * HALF : (h + 1) * HALF].rearrange(
                            "p c u d -> p c d u"
                        ),
                    )

        def quantise_weights(n):
            w_codes = codes_pool.tile(
                [P, UNIT_COLS], U32, name="w_codes", tag="w_codes", align_bytes=64
            )
            w_scales = codes_pool.tile(
                [P, UNIT_COLS], U8, name="w_scales", tag="w_scales", align_bytes=64
            )
            for part in range(2):
                cols = slice(part * UNIT_COLS // 2, (part + 1) * UNIT_COLS // 2)
                nc.vector.quantize_mx(
                    out=w_codes[:, cols].bitcast(FP8X4),
                    scales=w_scales[:, cols],
                    in_=w_grouped_tiles[n][:, cols.start * PACK : cols.stop * PACK],
                )
            w_quantised[n] = (w_codes, w_scales)

        def project(n, first=0, count=S, halves=(0, 1)):
            w_codes, w_scales = w_quantised[n]
            for h in halves:
                if first == 0:
                    acc_tiles[(n, h)] = acc_psum.tile([P, S], F32, name="acc", tag="acc")
                for g in range(PASSES):
                    cols = slice((2 * g + h) * P, (2 * g + h + 1) * P)
                    x_cols = slice(g * S + first, g * S + first + count)
                    nc.tensor.matmul_mx(
                        out=acc_tiles[(n, h)][:, first : first + count],
                        lhsT=w_codes[:, cols].bitcast(FP8X4),
                        lhsT_scale=w_scales[:, cols],
                        rhs=x_codes[:, x_cols].bitcast(FP8X4),
                        rhs_scale=x_scales[:, x_cols],
                        start=(g == 0),
                        stop=(g == PASSES - 1),
                    )

        rot_codes = []
        rot_scales = []
        for which in range(2):
            rot_codes.append(
                keep.tile([P, PASSES * S], U32, name="rot_codes%d" % which, align_bytes=64)
            )
            rot_scales.append(
                keep.tile([P, PASSES * S], U8, name="rot_scales%d" % which, align_bytes=64)
            )
        product_tiles = {}
        rot_tiles = {}
        rot_grouped_tiles = {}

        def rope_products(n, lo, hi, positions=slice(0, S)):
            if positions.start == 0:
                product_tiles[n] = rope_pool.tile([P, 4, S], F32, name="products", tag="products")
            products = product_tiles[n]
            twice = [P, 2, positions.stop - positions.start]
            nc.vector.tensor_tensor(
                out=products[:, 0:4:3, positions],
                in0=lo[:, positions].unsqueeze(1).to_broadcast(twice),
                in1=tables[:, COS_LO : SIN_HI + 1, positions],
                op=MULT,
            )
            nc.vector.tensor_tensor(
                out=products[:, 1:3, positions],
                in0=hi[:, positions].unsqueeze(1).to_broadcast(twice),
                in1=tables[:, COS_HI : NEG_SIN_LO + 1, positions],
                op=MULT,
            )

        def add_products(engine, n, first, end):
            out = rot_tiles[n // 2][:].rearrange("p (j s h) -> p j s h", j=2, h=2)[
                :, n % 2, first:end, :
            ]
            runs = product_tiles[n][:, :, first:end].rearrange("p t (c i) -> p c t i", i=4)
            engine.tensor_tensor(
                out=out.rearrange("p (c i) h -> p c h i", i=4),
                in0=runs[:, :, 0:2, :],
                in1=runs[:, :, 2:4, :],
                op=ADD,
            )

        def rope_sums(n):
            if n % 2 == 0:
                rot_tiles[n // 2] = rot_pool.tile([P, PACK * S], BF16, name="rot", tag="rot")
            if n == UNITS - 2:
                add_products(nc.gpsimd, n, 0, S)
                return
            add_products(nc.vector, n, GPSIMD_POSITIONS - FENCE, S)
            add_products(nc.gpsimd, n, 0, GPSIMD_POSITIONS)

        def group_rot(pair, copy=nc.scalar.copy, first=0, count=S):
            if first == 0:
                rot_grouped_tiles[pair] = rot_grouped_pool.tile(
                    [P, S * PACK], BF16, name="rot_grouped", tag="rot_grouped", align_bytes=64
                )
            words = rot_tiles[pair][:].bitcast(F32).rearrange("p (j s) -> p j s", j=2)
            grouped = rot_grouped_tiles[pair][:].bitcast(F32).rearrange("p (s j) -> p s j", j=2)
            copy(
                out=grouped[:, first : first + count, :],
                in_=words[:, :, first : first + count].rearrange("p j s -> p s j"),
            )

        def quantise_rot(pair, first=0, count=S):
            which = pair % 2
            cols = slice((pair // 2) * S + first, (pair // 2) * S + first + count)
            nc.vector.quantize_mx(
                out=rot_codes[which][:, cols].bitcast(FP8X4),
                scales=rot_scales[which][:, cols],
                in_=rot_grouped_tiles[pair][:, first * PACK : (first + count) * PACK],
            )

        def finish_rope(n):
            if 1 <= n <= UNITS:
                rope_sums(n - 1)
            if n % 2 == 1 and 3 <= n:
                group_rot((n - 3) // 2)

        keep_clock_up(acc_psum, "acc", 7)
        turn_tables(0, nc.vector.tensor_copy)
        turn_tables(1, nc.scalar.copy)
        keep_clock_up(acc_psum, "acc", 2)
        turn_weights(0, (nc.scalar.copy, nc.vector.tensor_copy))
        keep_clock_up(acc_psum, "acc", 2)
        turn_x(0, (nc.scalar.copy, nc.scalar.copy))
        turn_x(1, (nc.scalar.copy, nc.scalar.copy))
        keep_clock_up(acc_psum, "acc", 2)
        quantise_weights(0)
        quantise_x(0)
        turn_x(2, (nc.scalar.copy, nc.scalar.copy))
        quantise_x(1)
        turn_x(3, (nc.scalar.copy, nc.vector.tensor_copy))
        keep_clock_up(acc_psum, "acc", 2)
        quantise_x(2)
        quantise_x(3)
        turn_weights(1)
        project(0)
        for n in range(UNITS):
            if n + LOADS_AHEAD < UNITS:
                load_weights(n + LOADS_AHEAD)
            if n > 0:
                project(n)
            if 1 < n + 2 < UNITS:
                turn_weights(n + 2)
            if 0 < n + 1 < UNITS:
                quantise_weights(n + 1)
            finish_rope(n)
            if n < UNITS - 1:
                rope_products(n, acc_tiles[(n, 0)], acc_tiles[(n, 1)])
            if n % 2 == 0 and 4 <= n:
                quantise_rot((n - 4) // 2)

        n = UNITS - 1
        for half in range(2):
            positions = slice(half * (S // 2), (half + 1) * (S // 2))
            rope_products(n, acc_tiles[(n, 0)], acc_tiles[(n, 1)], positions)

        mask_sb = keep.tile([P, S_TILES, S], BF16, name="mask_sb")
        nc.sync.dma_start(out=mask_sb[:], in_=mask_rows.rearrange("(m p) s -> p m s", p=P))

        scores = {}

        def add_scores(g, half):
            for m in range(S_TILES):
                if g == 0:
                    pool, tag = ((turn_psum, "turn"), (acc_psum, "acc"))[half]
                    scores[(m, half)] = pool.tile([P, S // 2], F32, name="scores", tag=tag)
                q_cols = slice(g * S + m * P, g * S + (m + 1) * P)
                k_cols = slice(g * S + half * (S // 2), g * S + (half + 1) * (S // 2))
                nc.tensor.matmul_mx(
                    out=scores[(m, half)][:],
                    lhsT=rot_codes[0][:, q_cols].bitcast(FP8X4),
                    lhsT_scale=rot_scales[0][:, q_cols],
                    rhs=rot_codes[1][:, k_cols].bitcast(FP8X4),
                    rhs_scale=rot_scales[1][:, k_cols],
                    start=(g == 0),
                    stop=(g == PASSES - 1),
                )

        for h in range(2):
            for g in range(PASSES - 1):
                add_scores(g, h)
        half = S // 2
        add_products(nc.vector, UNITS - 1, 0, half)
        add_products(nc.vector, UNITS - 1, half, S)
        quantise_rot(UNITS // 2 - 2)
        group_rot(UNITS // 2 - 1, nc.scalar.copy, 0, half)
        group_rot(UNITS // 2 - 1, nc.scalar.copy, half, half)
        quantise_rot(UNITS // 2 - 1, 0, half)
        quantise_rot(UNITS // 2 - 1, half, half)
        for h in range(2):
            add_scores(PASSES - 1, h)
        results = []
        for h in range(2):
            for m in range(S_TILES):
                if h == 0:
                    results.append(out_pool.tile([P, S], F32, name="result", tag="result"))
                cols = slice(h * half, (h + 1) * half)
                nc.vector.scalar_tensor_tensor(
                    out=results[m][:, cols],
                    in0=scores[(m, h)][:],
                    scalar=1.0 / math.sqrt(HD),
                    in1=mask_sb[:, m, cols],
                    op0=MULT,
                    op1=ADD,
                )
                nc.sync.dma_start(
                    out=out_rows[m * P : (m + 1) * P, cols], in_=results[m][:, cols]
                )
